import numpy as np
import ml_dtypes


def mxq(x, axis, fmt="e4m3"):
    dtype, down = {"e4m3": (ml_dtypes.float8_e4m3fn, 7), "e5m2": (ml_dtypes.float8_e5m2, 14)}[fmt]
    v = np.moveaxis(np.asarray(x, np.float32).astype(ml_dtypes.bfloat16).astype(np.float64), axis, -1)
    blocks = v.reshape(v.shape[:-1] + (-1, 32))
    amax = np.abs(blocks).max(-1, keepdims=True)
    byte = np.maximum(np.where(amax > 0, np.frexp(amax)[1] - 1 + 127, 0) - down, 1)
    scale = np.exp2(byte - 127.0)
    codes = (blocks / scale).astype(np.float32).astype(dtype).astype(np.float64)
    return np.moveaxis((codes * scale).reshape(v.shape), -1, axis)


WIDE = False


def mx_kscale(k):
    if not WIDE:
        return np.ones(k)
    levels = np.array([10, -10, 5, -5, 0])
    a = np.random.permutation(np.resize(levels, k // 512 * 4)).reshape(k // 512, 4)
    idx = np.arange(k)
    return np.exp2(a[idx // 512, idx % 128 // 32])


BF16 = ml_dtypes.bfloat16


def bf(x):
    return np.asarray(x, np.float32).astype(BF16)


def f64(x):
    return np.asarray(x).astype(np.float64)


E2M1 = np.array([0.0, 0.5, 1.0, 1.5, 2.0, 3.0, 4.0, 6.0, -0.0, -0.5, -1.0, -1.5, -2.0, -3.0, -4.0, -6.0])


def pack_weight(w, fmt):
    k, n = w.shape
    w = f64(bf(w)).reshape(k // 32, 32, n)
    amax = np.abs(w).max(1)
    if fmt == "e4m3":
        byte = np.frexp(amax)[1] - 1 + 127 - 7
    else:
        mant, ex = np.frexp(amax / 6.0)
        byte = np.where(mant > 0.5, ex, ex - 1) + 127
    byte = np.clip(np.where(amax > 0, byte, 1), 1, 254)
    scaled = (w * np.exp2(127.0 - byte)[:, None, :]).reshape(k, n).astype(np.float32)
    by_word = np.ascontiguousarray(scaled.reshape(k // 512, 128, 4, n).transpose(0, 1, 3, 2))
    if fmt == "e4m3":
        words = by_word.astype(ml_dtypes.float8_e4m3fn).view(np.uint8)
    else:
        c = by_word.astype(ml_dtypes.float4_e2m1fn).view(np.uint8) & 0xF
        words = c[..., 0::2] | (c[..., 1::2] << 4)
    return np.ascontiguousarray(words), np.ascontiguousarray(byte.astype(np.uint8).reshape(k // 512, 16, n))


def unpack_weight(words, scales, fmt):
    g, p, n, _ = words.shape
    if fmt == "e4m3":
        vals = np.ascontiguousarray(words).view(ml_dtypes.float8_e4m3fn).astype(np.float64)
    else:
        nib = np.empty((g, p, n, 4), np.uint8)
        nib[..., 0::2] = words & 0xF
        nib[..., 1::2] = words >> 4
        vals = E2M1[nib]
    vals = vals * np.repeat(np.exp2(scales.astype(np.float64) - 127.0), 8, axis=1)[..., None]
    return vals.transpose(0, 1, 3, 2).reshape(g * 512, n)


B, T, N, C = 2, 2, 512, 1024
EDGE = 0.0625


def sigmoid(z):
    return 1.0 / (1.0 + np.exp(-z))


def setup_inputs():
    s = mx_kscale(C)
    x = bf(np.random.standard_normal((B, T, N, C)) * 0.5)
    hid = bf(np.maximum(np.random.standard_normal((B, T, N, C)), 0.0) * s)
    adj = bf(np.random.random((B, N, N)) * (np.random.random((B, N, N)) < EDGE))
    lam_raw = bf(3.5 + 0.1 * np.random.standard_normal(1))
    words, scales = pack_weight(np.random.standard_normal((C, C)) * 4.5 / np.sqrt(C) / s[:, None], "e4m3")
    return {"x": x,
            "hid": hid,
            "adj": adj,
            "lam_raw": lam_raw,
            "theta_words": words,
            "theta_scales": scales}


def reference(x, hid, adj, lam_raw, theta_words, theta_scales):
    lam = 1.0 + np.maximum(f64(lam_raw)[0], 0.0)
    h = mxq(f64(hid), 3, "e4m3") @ unpack_weight(theta_words, theta_scales, "e4m3")
    v = ((2.0 * lam - 2.0) / lam) * np.eye(N) + (2.0 / lam) * f64(adj)
    v = v / np.sum(v, axis=-1, keepdims=True)
    out = mxq(v, 2, "e4m3")[:, None] @ mxq(h, 2, "e4m3")
    return np.maximum(f64(x), 0.0) + sigmoid(np.maximum(out, 0.0))

@@ -1,0 +1,254 @@
+from contextlib import ExitStack
+
+import concourse.mybir as mybir
+from concourse.masks import make_identity
+
+F32 = mybir.dt.float32
+BF16 = mybir.dt.bfloat16
+I32 = mybir.dt.int32
+U32 = mybir.dt.uint32
+U8 = mybir.dt.uint8
+FP8X4 = mybir.dt.float8_e4m3fn_x4
+ALU = mybir.AluOpType
+ACT = mybir.ActivationFunctionType
+
+B, T, NODES, CH = 2, 2, 512, 1024
+P = 128
+PACK = 4
+K_PASS = P * PACK
+UNITS = B * T
+GROUPS = CH // K_PASS
+HALF = CH // 2
+HALVES = UNITS * 2
+BLOCK = P
+
+FLOPS = 2 * UNITS * NODES * CH * CH + 2 * UNITS * NODES * NODES * CH
+
+
+def tile_akgcn_pb_kernel(tc, x, hid, adj, lam_raw, theta_words, theta_scales, out):
+    nc = tc.nc
+    with ExitStack() as stack:
+        keep = stack.enter_context(tc.tile_pool(name="keep", bufs=1))
+        small = stack.enter_context(tc.tile_pool(name="small", bufs=4))
+        rows = stack.enter_context(tc.tile_pool(name="rows", bufs=4))
+        stage = stack.enter_context(tc.tile_pool(name="stage", bufs=2))
+        result = stack.enter_context(tc.tile_pool(name="result", bufs=4))
+        flip_psum = stack.enter_context(tc.psum_pool(name="flip_psum", bufs=2))
+        h_psum = stack.enter_context(tc.psum_pool(name="h_psum", bufs=3))
+        z_psum = stack.enter_context(tc.psum_pool(name="z_psum", bufs=3))
+
+        lam_bf = keep.tile([P, 1], BF16, name="lam_bf")
+        adj_sb = [keep.tile([P, PACK, NODES], BF16, name="adj%d" % b) for b in range(B)]
+        hid_sb = [keep.tile([P, PACK, CH], BF16, name="hid%d" % u) for u in range(UNITS)]
+        x_sb = [keep.tile([P, PACK, CH], BF16, name="x%d" % u) for u in range(UNITS)]
+        theta_codes = keep.tile([P, GROUPS, CH], U32, name="theta_codes", align_bytes=64)
+        theta_planes = keep.tile([P, GROUPS, CH], U8, name="theta_planes", align_bytes=64)
+        v_codes = [keep.tile([P, NODES], U32, name="v_codes%d" % b, align_bytes=64) for b in range(B)]
+        v_planes = [keep.tile([P, NODES], U8, name="v_planes%d" % b, align_bytes=64) for b in range(B)]
+
+        nc.vector.memset(theta_planes[:].bitcast(I32), 0)
+
+        nc.sync.dma_start(out=lam_bf[:], in_=lam_raw.partition_broadcast(P))
+
+        def load_adj(b):
+            nc.sync.dma_start(out=adj_sb[b][:], in_=adj[b].rearrange("(p i) m -> p i m", i=PACK))
+
+        def load_hid(u):
+            nc.sync.dma_start(out=hid_sb[u][:], in_=hid[u // T, u % T].rearrange("(p j) k -> p j k", j=PACK))
+
+        def load_x(u):
+            nc.sync.dma_start(out=x_sb[u][:], in_=x[u // T, u % T].rearrange("(p i) c -> p i c", i=PACK))
+
+        load_adj(0)
+        load_hid(0)
+        for quadrant in range(4):
+            nc.sync.dma_start(
+                out=theta_planes[32 * quadrant : 32 * quadrant + 4, :, :].bitcast(I32),
+                in_=theta_scales[:, 4 * quadrant : 4 * quadrant + 4, :].rearrange("g r n -> r g n").bitcast(I32),
+            )
+        for g in range(GROUPS):
+            nc.sync.dma_start(
+                out=theta_codes[:, g, :].bitcast(I32),
+                in_=theta_words[g].rearrange("p n t -> p (n t)").bitcast(I32),
+            )
+        load_hid(1)
+        load_adj(1)
+        load_x(0)
+        load_hid(2)
+        load_x(1)
+        load_hid(3)
+        load_x(2)
+        load_x(3)
+
+        ident_f32 = keep.tile([P, P], F32, name="ident_f32")
+        make_identity(nc, ident_f32[:])
+        eye_strip = keep.tile([P, 2 * PACK - 1, P], BF16, name="eye_strip")
+        nc.gpsimd.memset(eye_strip[:], 0.0)
+        make_identity(nc, eye_strip[:, PACK - 1, :])
+        ident_bf = eye_strip[:, PACK - 1, :]
+
+        warm = keep.tile([P, 1], F32, name="warm")
+        nc.vector.memset(warm[:], 0.0)
+        nc.scalar.activation(out=warm[:], in_=warm[:], func=ACT.Sigmoid)
+
+        r = keep.tile([P, 1], F32, name="r")
+        nc.vector.tensor_scalar_max(out=r[:], in0=lam_bf[:], scalar1=0.0)
+
+        v_rows = {}
+
+        def build_v_rows(b):
+            for i in range(PACK):
+                unscaled = rows.tile([P, PACK, P], F32, name="unscaled")
+                row_sum = small.tile([P, 1], F32, name="row_sum")
+                nc.vector.scalar_tensor_tensor(
+                    out=unscaled[:],
+                    in0=eye_strip[:, PACK - 1 - i : 2 * PACK - 1 - i, :],
+                    scalar=r[:, 0:1],
+                    in1=adj_sb[b][:, i, :].rearrange("p (q t) -> p t q", t=PACK),
+                    op0=ALU.mult,
+                    op1=ALU.add,
+                    accum_out=row_sum[:],
+                )
+                inverse = small.tile([P, 1], F32, name="inverse")
+                nc.vector.reciprocal(out=inverse[:], in_=row_sum[:])
+                scaled = rows.tile([P, PACK, P], BF16, name="scaled")
+                nc.vector.tensor_scalar(
+                    out=scaled[:], in0=unscaled[:], scalar1=inverse[:, 0:1], scalar2=None, op0=ALU.mult
+                )
+                v_rows[(b, i)] = scaled
+
+        def transpose_v(b):
+            v_grouped = stage.tile([P, PACK, P, PACK], BF16, name="v_grouped", align_bytes=64)
+            for i in range(PACK):
+                flipped = flip_psum.tile([P, PACK, P], BF16, name="flipped_v", tag="flip")
+                for t in range(PACK):
+                    nc.tensor.transpose(flipped[:, t, :], v_rows[(b, i)][:, t, :], ident_bf)
+                nc.scalar.copy(out=v_grouped[:, i, :, :], in_=flipped[:].rearrange("q t p -> q p t"))
+            nc.vector.quantize_mx(
+                out=v_codes[b][:].bitcast(FP8X4),
+                scales=v_planes[b][:],
+                in_=v_grouped[:].rearrange("q i p t -> q (i p t)"),
+            )
+
+        hid_codes = {}
+        hid_planes = {}
+
+        def transpose_hid(u):
+            hid_grouped = stage.tile([P, PACK, GROUPS, P, PACK], BF16, name="hid_grouped", align_bytes=64)
+            for j in range(PACK):
+                words = hid_sb[u][:, j, :].bitcast(F32)
+                flipped = flip_psum.tile([P, GROUPS, 2, P], F32, name="flipped_hid", tag="flip")
+                for g in range(GROUPS):
+                    for pair in range(2):
+                        nc.tensor.transpose(
+                            flipped[:, g, pair, :],
+                            words[:, 256 * g + pair : 256 * (g + 1) : 2],
+                            ident_f32[:],
+                        )
+                target = hid_grouped[:, j, :, :, :].bitcast(F32)
+                source = flipped[:].rearrange("p g pair n -> p g n pair")
+                if j % 2 == 0:
+                    nc.scalar.copy(out=target, in_=source)
+                else:
+                    nc.vector.tensor_copy(out=target, in_=source)
+            codes = stage.tile([P, PACK * GROUPS * P], U32, name="hid_codes", align_bytes=64)
+            planes = stage.tile([P, PACK * GROUPS * P], U8, name="hid_planes", align_bytes=64)
+            nc.vector.quantize_mx(
+                out=codes[:].bitcast(FP8X4),
+                scales=planes[:],
+                in_=hid_grouped[:].rearrange("p j g n t -> p (j g n t)"),
+            )
+            hid_codes[u] = codes
+            hid_planes[u] = planes
+
+        h_grouped = {}
+        h_codes = {}
+        h_planes = {}
+
+        def first_matmul(hu, step):
+            u, half = divmod(hu, 2)
+            if step == 0:
+                h_grouped[hu] = stage.tile([P, HALF, PACK], BF16, name="h_grouped", align_bytes=64)
+            first = HALF * half + BLOCK * step
+            bank = h_psum.tile([P, PACK, BLOCK], F32, name="h_bank")
+            for j in range(PACK):
+                for g in range(GROUPS):
+                    nodes = slice((j * GROUPS + g) * P, (j * GROUPS + g + 1) * P)
+                    nc.tensor.matmul_mx(
+                        out=bank[:, j, :],
+                        lhsT=hid_codes[u][:, nodes].bitcast(FP8X4),
+                        lhsT_scale=hid_planes[u][:, nodes],
+                        rhs=theta_codes[:, g, first : first + BLOCK].bitcast(FP8X4),
+                        rhs_scale=theta_planes[:, g, first : first + BLOCK],
+                        start=(g == 0),
+                        stop=(g == GROUPS - 1),
+                    )
+            nc.scalar.copy(
+                out=h_grouped[hu][:, BLOCK * step : BLOCK * (step + 1), :],
+                in_=bank[:].rearrange("p j c -> p c j"),
+            )
+
+        def quantise_h(hu):
+            codes = stage.tile([P, HALF], U32, name="h_codes", align_bytes=64)
+            planes = stage.tile([P, HALF], U8, name="h_planes", align_bytes=64)
+            nc.vector.quantize_mx(
+                out=codes[:].bitcast(FP8X4),
+                scales=planes[:],
+                in_=h_grouped[hu][:].rearrange("p c j -> p (c j)"),
+            )
+            h_codes[hu] = codes
+            h_planes[hu] = planes
+
+        def relu_x(u):
+            flat = x_sb[u][:].rearrange("p i c -> p (i c)")
+            nc.vector.tensor_scalar_max(out=flat, in0=flat, scalar1=0.0)
+
+        def second_matmul(hu, i):
+            u, half = divmod(hu, 2)
+            b = u // T
+            channels = slice(HALF * half, HALF * (half + 1))
+            bank = z_psum.tile([P, HALF], F32, name="z_bank")
+            nc.tensor.matmul_mx(
+                out=bank[:],
+                lhsT=v_codes[b][:, P * i : P * (i + 1)].bitcast(FP8X4),
+                lhsT_scale=v_planes[b][:, P * i : P * (i + 1)],
+                rhs=h_codes[hu][:].bitcast(FP8X4),
+                rhs_scale=h_planes[hu][:],
+                start=True,
+                stop=True,
+            )
+            gate = result.tile([P, HALF], F32, name="gate")
+            nc.scalar.activation(out=gate[:], in_=bank[:], func=ACT.Sigmoid)
+            total = result.tile([P, HALF], F32, name="total")
+            nc.vector.scalar_tensor_tensor(
+                out=total[:],
+                in0=gate[:],
+                scalar=0.5,
+                in1=x_sb[u][:, i, channels],
+                op0=ALU.max,
+                op1=ALU.add,
+            )
+            nc.sync.dma_start(
+                out=out[u // T, u % T].rearrange("(p i) c -> p i c", i=PACK)[:, i, channels],
+                in_=total[:],
+            )
+
+        build_v_rows(0)
+        transpose_hid(0)
+        for hu in range(HALVES):
+            u, half = divmod(hu, 2)
+            if half == 0 and u < B:
+                transpose_v(u)
+            if half == 1 and u + 1 < UNITS:
+                transpose_hid(u + 1)
+            for step in range(PACK):
+                first_matmul(hu, step)
+                if hu > 0:
+                    second_matmul(hu - 1, step)
+            quantise_h(hu)
+            if half == 0:
+                relu_x(u)
+            if half == 0 and u + 1 < B:
+                build_v_rows(u + 1)
+        for step in range(PACK):
+            second_matmul(HALVES - 1, step)

@@ -19,8 +19,12 @@ K_PASS = P * PACK
 UNITS = B * T
 GROUPS = CH // K_PASS
 HALF = CH // 2
-HALVES = UNITS * 2
 BLOCK = P
+STEPS = UNITS * CH // BLOCK
+STEPS_PER_HALF = HALF // BLOCK
+STEPS_PER_UNIT = CH // BLOCK
+STEPS_PER_BATCH = T * STEPS_PER_UNIT
+LAG = 6
 
 FLOPS = 2 * UNITS * NODES * CH * CH + 2 * UNITS * NODES * NODES * CH
 
@@ -32,10 +36,8 @@ def tile_akgcn_pb_kernel(tc, x, hid, adj, lam_raw, theta_words, theta_scales, ou
         small = stack.enter_context(tc.tile_pool(name="small", bufs=4))
         rows = stack.enter_context(tc.tile_pool(name="rows", bufs=4))
         stage = stack.enter_context(tc.tile_pool(name="stage", bufs=2))
-        result = stack.enter_context(tc.tile_pool(name="result", bufs=4))
-        flip_psum = stack.enter_context(tc.psum_pool(name="flip_psum", bufs=2))
-        h_psum = stack.enter_context(tc.psum_pool(name="h_psum", bufs=3))
-        z_psum = stack.enter_context(tc.psum_pool(name="z_psum", bufs=3))
+        result = stack.enter_context(tc.tile_pool(name="result", bufs=6))
+        banks = stack.enter_context(tc.psum_pool(name="banks", bufs=8))
 
         lam_bf = keep.tile([P, 1], BF16, name="lam_bf")
         adj_sb = [keep.tile([P, PACK, NODES], BF16, name="adj%d" % b) for b in range(B)]
@@ -60,32 +62,38 @@ def tile_akgcn_pb_kernel(tc, x, hid, adj, lam_raw, theta_words, theta_scales, ou
             nc.sync.dma_start(out=x_sb[u][:], in_=x[u // T, u % T].rearrange("(p i) c -> p i c", i=PACK))
 
         load_adj(0)
-        load_hid(0)
+        for j in range(PACK):
+            nc.sync.dma_start(
+                out=hid_sb[0][:, j, :], in_=hid[0, 0].rearrange("(p j) k -> p j k", j=PACK)[:, j, :]
+            )
         for quadrant in range(4):
             nc.sync.dma_start(
                 out=theta_planes[32 * quadrant : 32 * quadrant + 4, :, :].bitcast(I32),
                 in_=theta_scales[:, 4 * quadrant : 4 * quadrant + 4, :].rearrange("g r n -> r g n").bitcast(I32),
             )
-        for g in range(GROUPS):
-            nc.sync.dma_start(
-                out=theta_codes[:, g, :].bitcast(I32),
-                in_=theta_words[g].rearrange("p n t -> p (n t)").bitcast(I32),
-            )
+        for half in range(2):
+            for g in range(GROUPS):
+                nc.sync.dma_start(
+                    out=theta_codes[:, g, HALF * half : HALF * (half + 1)].bitcast(I32),
+                    in_=theta_words[g, :, HALF * half : HALF * (half + 1), :]
+                    .rearrange("p n t -> p (n t)")
+                    .bitcast(I32),
+                )
         load_hid(1)
-        load_adj(1)
         load_x(0)
+        load_adj(1)
         load_hid(2)
         load_x(1)
         load_hid(3)
         load_x(2)
         load_x(3)
 
-        ident_f32 = keep.tile([P, P], F32, name="ident_f32")
-        make_identity(nc, ident_f32[:])
         eye_strip = keep.tile([P, 2 * PACK - 1, P], BF16, name="eye_strip")
         nc.gpsimd.memset(eye_strip[:], 0.0)
         make_identity(nc, eye_strip[:, PACK - 1, :])
         ident_bf = eye_strip[:, PACK - 1, :]
+        ident_f32 = keep.tile([P, P], F32, name="ident_f32")
+        make_identity(nc, ident_f32[:])
 
         warm = keep.tile([P, 1], F32, name="warm")
         nc.vector.memset(warm[:], 0.0)
@@ -96,118 +104,114 @@ def tile_akgcn_pb_kernel(tc, x, hid, adj, lam_raw, theta_words, theta_scales, ou
 
         v_rows = {}
 
-        def build_v_rows(b):
-            for i in range(PACK):
-                unscaled = rows.tile([P, PACK, P], F32, name="unscaled")
-                row_sum = small.tile([P, 1], F32, name="row_sum")
-                nc.vector.scalar_tensor_tensor(
-                    out=unscaled[:],
-                    in0=eye_strip[:, PACK - 1 - i : 2 * PACK - 1 - i, :],
-                    scalar=r[:, 0:1],
-                    in1=adj_sb[b][:, i, :].rearrange("p (q t) -> p t q", t=PACK),
-                    op0=ALU.mult,
-                    op1=ALU.add,
-                    accum_out=row_sum[:],
-                )
-                inverse = small.tile([P, 1], F32, name="inverse")
-                nc.vector.reciprocal(out=inverse[:], in_=row_sum[:])
-                scaled = rows.tile([P, PACK, P], BF16, name="scaled")
-                nc.vector.tensor_scalar(
-                    out=scaled[:], in0=unscaled[:], scalar1=inverse[:, 0:1], scalar2=None, op0=ALU.mult
-                )
-                v_rows[(b, i)] = scaled
+        def build_v_rows(b, i):
+            unscaled = rows.tile([P, PACK, P], F32, name="unscaled")
+            row_sum = small.tile([P, 1], F32, name="row_sum")
+            nc.vector.scalar_tensor_tensor(
+                out=unscaled[:],
+                in0=eye_strip[:, PACK - 1 - i : 2 * PACK - 1 - i, :],
+                scalar=r[:, 0:1],
+                in1=adj_sb[b][:, i, :].rearrange("p (q t) -> p t q", t=PACK),
+                op0=ALU.mult,
+                op1=ALU.add,
+                accum_out=row_sum[:],
+            )
+            inverse = small.tile([P, 1], F32, name="inverse")
+            nc.vector.reciprocal(out=inverse[:], in_=row_sum[:])
+            scaled = rows.tile([P, PACK, P], BF16, name="scaled")
+            nc.scalar.activation(out=scaled[:], in_=unscaled[:], func=ACT.Copy, scale=inverse[:, 0:1])
+            v_rows[(b, i)] = scaled
 
         def transpose_v(b):
             v_grouped = stage.tile([P, PACK, P, PACK], BF16, name="v_grouped", align_bytes=64)
             for i in range(PACK):
-                flipped = flip_psum.tile([P, PACK, P], BF16, name="flipped_v", tag="flip")
+                flipped = banks.tile([P, PACK, P], BF16, name="flipped_v", tag="bank")
                 for t in range(PACK):
                     nc.tensor.transpose(flipped[:, t, :], v_rows[(b, i)][:, t, :], ident_bf)
-                nc.scalar.copy(out=v_grouped[:, i, :, :], in_=flipped[:].rearrange("q t p -> q p t"))
+                nc.vector.tensor_copy(out=v_grouped[:, i, :, :], in_=flipped[:].rearrange("q t p -> q p t"))
             nc.vector.quantize_mx(
                 out=v_codes[b][:].bitcast(FP8X4),
                 scales=v_planes[b][:],
                 in_=v_grouped[:].rearrange("q i p t -> q (i p t)"),
             )
 
+        hid_grouped = {}
         hid_codes = {}
         hid_planes = {}
 
-        def transpose_hid(u):
-            hid_grouped = stage.tile([P, PACK, GROUPS, P, PACK], BF16, name="hid_grouped", align_bytes=64)
-            for j in range(PACK):
-                words = hid_sb[u][:, j, :].bitcast(F32)
-                flipped = flip_psum.tile([P, GROUPS, 2, P], F32, name="flipped_hid", tag="flip")
-                for g in range(GROUPS):
-                    for pair in range(2):
-                        nc.tensor.transpose(
-                            flipped[:, g, pair, :],
-                            words[:, 256 * g + pair : 256 * (g + 1) : 2],
-                            ident_f32[:],
-                        )
-                target = hid_grouped[:, j, :, :, :].bitcast(F32)
-                source = flipped[:].rearrange("p g pair n -> p g n pair")
-                if j % 2 == 0:
-                    nc.scalar.copy(out=target, in_=source)
-                else:
-                    nc.vector.tensor_copy(out=target, in_=source)
-            codes = stage.tile([P, PACK * GROUPS * P], U32, name="hid_codes", align_bytes=64)
-            planes = stage.tile([P, PACK * GROUPS * P], U8, name="hid_planes", align_bytes=64)
+        def flip_hid(u, j):
+            if j == 0:
+                hid_grouped[u] = stage.tile([P, PACK, GROUPS * P * PACK], BF16, name="hid_grouped", align_bytes=64)
+                hid_codes[u] = stage.tile([P, PACK, GROUPS * P], U32, name="hid_codes", align_bytes=64)
+                hid_planes[u] = stage.tile([P, PACK, GROUPS * P], U8, name="hid_planes", align_bytes=64)
+            words = hid_sb[u][:, j, :].bitcast(F32)
+            flipped = banks.tile([P, GROUPS, 2, P], F32, name="flipped_hid", tag="bank")
+            for g in range(GROUPS):
+                for pair in range(2):
+                    nc.tensor.transpose(
+                        flipped[:, g, pair, :],
+                        words[:, 256 * g + pair : 256 * (g + 1) : 2],
+                        ident_f32[:],
+                    )
+            target = hid_grouped[u][:, j, :].bitcast(F32).rearrange("p (g n pair) -> p g n pair", g=GROUPS, pair=2)
+            source = flipped[:].rearrange("p g pair n -> p g n pair")
+            if j % 2 == 0:
+                nc.scalar.copy(out=target, in_=source)
+            else:
+                nc.vector.tensor_copy(out=target, in_=source)
+
+        def quantise_hid(u, j):
             nc.vector.quantize_mx(
-                out=codes[:].bitcast(FP8X4),
-                scales=planes[:],
-                in_=hid_grouped[:].rearrange("p j g n t -> p (j g n t)"),
+                out=hid_codes[u][:, j, :].bitcast(FP8X4),
+                scales=hid_planes[u][:, j, :],
+                in_=hid_grouped[u][:, j, :],
             )
-            hid_codes[u] = codes
-            hid_planes[u] = planes
 
         h_grouped = {}
         h_codes = {}
         h_planes = {}
 
-        def first_matmul(hu, step):
-            u, half = divmod(hu, 2)
-            if step == 0:
+        def first_matmul(s):
+            u, block = divmod(s, STEPS_PER_UNIT)
+            hu, quarter = divmod(s, STEPS_PER_HALF)
+            if quarter == 0:
                 h_grouped[hu] = stage.tile([P, HALF, PACK], BF16, name="h_grouped", align_bytes=64)
-            first = HALF * half + BLOCK * step
-            bank = h_psum.tile([P, PACK, BLOCK], F32, name="h_bank")
+            bank = banks.tile([P, PACK, BLOCK], F32, name="h_bank", tag="bank")
             for j in range(PACK):
                 for g in range(GROUPS):
-                    nodes = slice((j * GROUPS + g) * P, (j * GROUPS + g + 1) * P)
                     nc.tensor.matmul_mx(
                         out=bank[:, j, :],
-                        lhsT=hid_codes[u][:, nodes].bitcast(FP8X4),
-                        lhsT_scale=hid_planes[u][:, nodes],
-                        rhs=theta_codes[:, g, first : first + BLOCK].bitcast(FP8X4),
-                        rhs_scale=theta_planes[:, g, first : first + BLOCK],
+                        lhsT=hid_codes[u][:, j, P * g : P * (g + 1)].bitcast(FP8X4),
+                        lhsT_scale=hid_planes[u][:, j, P * g : P * (g + 1)],
+                        rhs=theta_codes[:, g, BLOCK * block : BLOCK * (block + 1)].bitcast(FP8X4),
+                        rhs_scale=theta_planes[:, g, BLOCK * block : BLOCK * (block + 1)],
                         start=(g == 0),
                         stop=(g == GROUPS - 1),
                     )
             nc.scalar.copy(
-                out=h_grouped[hu][:, BLOCK * step : BLOCK * (step + 1), :],
+                out=h_grouped[hu][:, BLOCK * quarter : BLOCK * (quarter + 1), :],
                 in_=bank[:].rearrange("p j c -> p c j"),
             )
 
         def quantise_h(hu):
-            codes = stage.tile([P, HALF], U32, name="h_codes", align_bytes=64)
-            planes = stage.tile([P, HALF], U8, name="h_planes", align_bytes=64)
+            h_codes[hu] = stage.tile([P, HALF], U32, name="h_codes", align_bytes=64, bufs=3)
+            h_planes[hu] = stage.tile([P, HALF], U8, name="h_planes", align_bytes=64, bufs=3)
             nc.vector.quantize_mx(
-                out=codes[:].bitcast(FP8X4),
-                scales=planes[:],
+                out=h_codes[hu][:].bitcast(FP8X4),
+                scales=h_planes[hu][:],
                 in_=h_grouped[hu][:].rearrange("p c j -> p (c j)"),
             )
-            h_codes[hu] = codes
-            h_planes[hu] = planes
 
         def relu_x(u):
             flat = x_sb[u][:].rearrange("p i c -> p (i c)")
             nc.vector.tensor_scalar_max(out=flat, in0=flat, scalar1=0.0)
 
-        def second_matmul(hu, i):
+        def second_matmul(s):
+            hu, i = divmod(s, STEPS_PER_HALF)
             u, half = divmod(hu, 2)
             b = u // T
             channels = slice(HALF * half, HALF * (half + 1))
-            bank = z_psum.tile([P, HALF], F32, name="z_bank")
+            bank = banks.tile([P, HALF], F32, name="z_bank", tag="bank")
             nc.tensor.matmul_mx(
                 out=bank[:],
                 lhsT=v_codes[b][:, P * i : P * (i + 1)].bitcast(FP8X4),
@@ -233,22 +237,32 @@ def tile_akgcn_pb_kernel(tc, x, hid, adj, lam_raw, theta_words, theta_scales, ou
                 in_=total[:],
             )
 
-        build_v_rows(0)
-        transpose_hid(0)
-        for hu in range(HALVES):
-            u, half = divmod(hu, 2)
-            if half == 0 and u < B:
-                transpose_v(u)
-            if half == 1 and u + 1 < UNITS:
-                transpose_hid(u + 1)
-            for step in range(PACK):
-                first_matmul(hu, step)
-                if hu > 0:
-                    second_matmul(hu - 1, step)
-            quantise_h(hu)
-            if half == 0:
-                relu_x(u)
-            if half == 0 and u + 1 < B:
-                build_v_rows(u + 1)
-        for step in range(PACK):
-            second_matmul(HALVES - 1, step)
+        for j in range(PACK):
+            build_v_rows(0, j)
+            flip_hid(0, j)
+            if j > 0:
+                quantise_hid(0, j - 1)
+        quantise_hid(0, PACK - 1)
+        transpose_v(0)
+
+        for s in range(STEPS + LAG):
+            next_unit = s // STEPS_PER_UNIT + 1
+            if s % STEPS_PER_UNIT == STEPS_PER_HALF and next_unit < UNITS:
+                for j in range(PACK):
+                    flip_hid(next_unit, j)
+                for j in range(PACK):
+                    quantise_hid(next_unit, j)
+            next_batch = s // STEPS_PER_BATCH + 1
+            row = s % STEPS_PER_BATCH - STEPS_PER_UNIT
+            if 0 <= row < PACK and next_batch < B:
+                build_v_rows(next_batch, row)
+            if s % STEPS_PER_BATCH == 0 and 0 < s < STEPS:
+                transpose_v(s // STEPS_PER_BATCH)
+            if (s + 1 - LAG) % STEPS_PER_UNIT == 0 and s + 1 - LAG < STEPS:
+                relu_x((s + 1 - LAG) // STEPS_PER_UNIT)
+            if s < STEPS:
+                first_matmul(s)
+            if s >= LAG:
+                second_matmul(s - LAG)
+            if s < STEPS and s % STEPS_PER_HALF == STEPS_PER_HALF - 1:
+                quantise_h(s // STEPS_PER_HALF)

@@ -119,7 +119,7 @@ def tile_akgcn_pb_kernel(tc, x, hid, adj, lam_raw, theta_words, theta_scales, ou
             inverse = small.tile([P, 1], F32, name="inverse")
             nc.vector.reciprocal(out=inverse[:], in_=row_sum[:])
             scaled = rows.tile([P, PACK, P], BF16, name="scaled")
-            nc.scalar.activation(out=scaled[:], in_=unscaled[:], func=ACT.Copy, scale=inverse[:, 0:1])
+            nc.vector.tensor_scalar_mul(out=scaled[:], in0=unscaled[:], scalar1=inverse[:, 0:1])
             v_rows[(b, i)] = scaled
 
         def transpose_v(b):
@@ -155,10 +155,7 @@ def tile_akgcn_pb_kernel(tc, x, hid, adj, lam_raw, theta_words, theta_scales, ou
                     )
             target = hid_grouped[u][:, j, :].bitcast(F32).rearrange("p (g n pair) -> p g n pair", g=GROUPS, pair=2)
             source = flipped[:].rearrange("p g pair n -> p g n pair")
-            if j % 2 == 0:
-                nc.scalar.copy(out=target, in_=source)
-            else:
-                nc.vector.tensor_copy(out=target, in_=source)
+            nc.scalar.copy(out=target, in_=source)
 
         def quantise_hid(u, j):
             nc.vector.quantize_mx(

@@ -102,33 +102,52 @@ def tile_akgcn_pb_kernel(tc, x, hid, adj, lam_raw, theta_words, theta_scales, ou
         r = keep.tile([P, 1], F32, name="r")
         nc.vector.tensor_scalar_max(out=r[:], in0=lam_bf[:], scalar1=0.0)
 
-        v_rows = {}
+        unscaled_rows = {}
+        row_sums = {}
 
-        def build_v_rows(b, i):
-            unscaled = rows.tile([P, PACK, P], F32, name="unscaled")
-            row_sum = small.tile([P, 1], F32, name="row_sum")
+        def sum_v_rows(b, i):
+            if i == 0:
+                row_sums[b] = small.tile([P, PACK], F32, name="row_sums")
+            unscaled_rows[(b, i)] = rows.tile([P, PACK, P], F32, name="unscaled")
             nc.vector.scalar_tensor_tensor(
-                out=unscaled[:],
+                out=unscaled_rows[(b, i)][:],
                 in0=eye_strip[:, PACK - 1 - i : 2 * PACK - 1 - i, :],
                 scalar=r[:, 0:1],
                 in1=adj_sb[b][:, i, :].rearrange("p (q t) -> p t q", t=PACK),
                 op0=ALU.mult,
                 op1=ALU.add,
-                accum_out=row_sum[:],
+                accum_out=row_sums[b][:, i : i + 1],
             )
-            inverse = small.tile([P, 1], F32, name="inverse")
-            nc.vector.reciprocal(out=inverse[:], in_=row_sum[:])
-            scaled = rows.tile([P, PACK, P], BF16, name="scaled")
-            nc.vector.tensor_scalar_mul(out=scaled[:], in0=unscaled[:], scalar1=inverse[:, 0:1])
-            v_rows[(b, i)] = scaled
+
+        inverses = {}
+        scaled_rows = {}
+
+        def invert_row_sums(b, first, count):
+            if first == 0:
+                inverses[b] = small.tile([P, PACK], F32, name="inverse")
+            nc.vector.reciprocal(out=inverses[b][:, first : first + count], in_=row_sums[b][:, first : first + count])
+
+        def scale_v_rows(b, i):
+            scaled_rows[(b, i)] = rows.tile([P, PACK, P], BF16, name="scaled")
+            if b == 0:
+                nc.scalar.activation(
+                    out=scaled_rows[(b, i)][:], in_=unscaled_rows[(b, i)][:], func=ACT.Copy, scale=inverses[b][:, i : i + 1]
+                )
+            else:
+                nc.vector.tensor_scalar_mul(
+                    out=scaled_rows[(b, i)][:], in0=unscaled_rows[(b, i)][:], scalar1=inverses[b][:, i : i + 1]
+                )
 
         def transpose_v(b):
             v_grouped = stage.tile([P, PACK, P, PACK], BF16, name="v_grouped", align_bytes=64)
-            for i in range(PACK):
-                flipped = banks.tile([P, PACK, P], BF16, name="flipped_v", tag="bank")
-                for t in range(PACK):
-                    nc.tensor.transpose(flipped[:, t, :], v_rows[(b, i)][:, t, :], ident_bf)
-                nc.vector.tensor_copy(out=v_grouped[:, i, :, :], in_=flipped[:].rearrange("q t p -> q p t"))
+            for pair in range(PACK // 2):
+                flipped = banks.tile([P, 2, PACK, P], BF16, name="flipped_v", tag="bank")
+                for k in range(2):
+                    for t in range(PACK):
+                        nc.tensor.transpose(flipped[:, k, t, :], scaled_rows[(b, 2 * pair + k)][:, t, :], ident_bf)
+                nc.vector.tensor_copy(
+                    out=v_grouped[:, 2 * pair : 2 * pair + 2, :, :], in_=flipped[:].rearrange("q k t p -> q k p t")
+                )
             nc.vector.quantize_mx(
                 out=v_codes[b][:].bitcast(FP8X4),
                 scales=v_planes[b][:],
@@ -155,13 +174,23 @@ def tile_akgcn_pb_kernel(tc, x, hid, adj, lam_raw, theta_words, theta_scales, ou
                     )
             target = hid_grouped[u][:, j, :].bitcast(F32).rearrange("p (g n pair) -> p g n pair", g=GROUPS, pair=2)
             source = flipped[:].rearrange("p g pair n -> p g n pair")
-            nc.scalar.copy(out=target, in_=source)
+            if j == PACK - 1 and u > 0:
+                nc.vector.tensor_copy(out=target, in_=source)
+            else:
+                nc.scalar.copy(out=target, in_=source)
 
         def quantise_hid(u, j):
             nc.vector.quantize_mx(
                 out=hid_codes[u][:, j, :].bitcast(FP8X4),
                 scales=hid_planes[u][:, j, :],
                 in_=hid_grouped[u][:, j, :],
+            )
+
+        def quantise_hid_whole(u):
+            nc.vector.quantize_mx(
+                out=hid_codes[u][:].rearrange("p j n -> p (j n)").bitcast(FP8X4),
+                scales=hid_planes[u][:].rearrange("p j n -> p (j n)"),
+                in_=hid_grouped[u][:].rearrange("p j n -> p (j n)"),
             )
 
         h_grouped = {}
@@ -203,6 +232,8 @@ def tile_akgcn_pb_kernel(tc, x, hid, adj, lam_raw, theta_words, theta_scales, ou
             flat = x_sb[u][:].rearrange("p i c -> p (i c)")
             nc.vector.tensor_scalar_max(out=flat, in0=flat, scalar1=0.0)
 
+        gates = [None]
+
         def second_matmul(s):
             hu, i = divmod(s, STEPS_PER_HALF)
             u, half = divmod(hu, 2)
@@ -218,24 +249,34 @@ def tile_akgcn_pb_kernel(tc, x, hid, adj, lam_raw, theta_words, theta_scales, ou
                 start=True,
                 stop=True,
             )
-            gate = result.tile([P, HALF], F32, name="gate")
-            nc.scalar.activation(out=gate[:], in_=bank[:], func=ACT.Sigmoid)
-            total = result.tile([P, HALF], F32, name="total")
+            if i % 2 == 0:
+                gates[0] = result.tile([P, 2, HALF], F32, name="gate")
+            gate = gates[0]
+            nc.scalar.activation(out=gate[:, i % 2, :], in_=bank[:], func=ACT.Sigmoid)
+            if s >= STEPS - 2:
+                first, count = i, 1
+            elif i % 2 == 1:
+                first, count = i - 1, 2
+            else:
+                return
+            total = result.tile([P, 2, HALF], F32, name="total")
             nc.vector.scalar_tensor_tensor(
-                out=total[:],
-                in0=gate[:],
+                out=total[:, 0:count, :],
+                in0=gate[:, first % 2 : first % 2 + count, :],
                 scalar=0.5,
-                in1=x_sb[u][:, i, channels],
+                in1=x_sb[u][:, first : first + count, channels],
                 op0=ALU.max,
                 op1=ALU.add,
             )
             nc.sync.dma_start(
-                out=out[u // T, u % T].rearrange("(p i) c -> p i c", i=PACK)[:, i, channels],
-                in_=total[:],
+                out=out[u // T, u % T].rearrange("(p i) c -> p i c", i=PACK)[:, first : first + count, channels],
+                in_=total[:, 0:count, :],
             )
 
         for j in range(PACK):
-            build_v_rows(0, j)
+            sum_v_rows(0, j)
+            invert_row_sums(0, j, 1)
+            scale_v_rows(0, j)
             flip_hid(0, j)
             if j > 0:
                 quantise_hid(0, j - 1)
@@ -247,12 +288,15 @@ def tile_akgcn_pb_kernel(tc, x, hid, adj, lam_raw, theta_words, theta_scales, ou
             if s % STEPS_PER_UNIT == STEPS_PER_HALF and next_unit < UNITS:
                 for j in range(PACK):
                     flip_hid(next_unit, j)
-                for j in range(PACK):
-                    quantise_hid(next_unit, j)
+                quantise_hid_whole(next_unit)
             next_batch = s // STEPS_PER_BATCH + 1
             row = s % STEPS_PER_BATCH - STEPS_PER_UNIT
             if 0 <= row < PACK and next_batch < B:
-                build_v_rows(next_batch, row)
+                sum_v_rows(next_batch, row)
+            if row == PACK and next_batch < B:
+                invert_row_sums(next_batch, 0, PACK)
+            if PACK <= row < 2 * PACK and next_batch < B:
+                scale_v_rows(next_batch, row - PACK)
             if s % STEPS_PER_BATCH == 0 and 0 < s < STEPS:
                 transpose_v(s // STEPS_PER_BATCH)
             if (s + 1 - LAG) % STEPS_PER_UNIT == 0 and s + 1 - LAG < STEPS:

@@ -25,6 +25,11 @@ STEPS_PER_HALF = HALF // BLOCK
 STEPS_PER_UNIT = CH // BLOCK
 STEPS_PER_BATCH = T * STEPS_PER_UNIT
 LAG = 6
+HC_V = (25, 29)
+FLIP_V = ((1, 3), (2, 3), (3, 3))
+SINGLE_FROM = 28
+ADJ_PIECES = 1
+WARM = 0
 
 FLOPS = 2 * UNITS * NODES * CH * CH + 2 * UNITS * NODES * NODES * CH
 
@@ -61,7 +66,12 @@ def tile_akgcn_pb_kernel(tc, x, hid, adj, lam_raw, theta_words, theta_scales, ou
         def load_x(u):
             nc.sync.dma_start(out=x_sb[u][:], in_=x[u // T, u % T].rearrange("(p i) c -> p i c", i=PACK))
 
-        load_adj(0)
+        for piece in range(ADJ_PIECES):
+            span = PACK // ADJ_PIECES
+            nc.sync.dma_start(
+                out=adj_sb[0][:, span * piece : span * (piece + 1), :],
+                in_=adj[0].rearrange("(p i) m -> p i m", i=PACK)[:, span * piece : span * (piece + 1), :],
+            )
         for j in range(PACK):
             nc.sync.dma_start(
                 out=hid_sb[0][:, j, :], in_=hid[0, 0].rearrange("(p j) k -> p j k", j=PACK)[:, j, :]
@@ -94,6 +104,13 @@ def tile_akgcn_pb_kernel(tc, x, hid, adj, lam_raw, theta_words, theta_scales, ou
         ident_bf = eye_strip[:, PACK - 1, :]
         ident_f32 = keep.tile([P, P], F32, name="ident_f32")
         make_identity(nc, ident_f32[:])
+
+        if WARM:
+            idle_rows = keep.tile([P, HALF], BF16, name="idle_rows")
+            nc.vector.memset(idle_rows[:], 0.0)
+            idle_bank = banks.tile([P, HALF], F32, name="idle_bank", tag="bank")
+            for repeat in range(WARM):
+                nc.tensor.matmul(out=idle_bank[:], lhsT=idle_rows[:, 0:P], rhs=idle_rows[:], start=True, stop=True)
 
         warm = keep.tile([P, 1], F32, name="warm")
         nc.vector.memset(warm[:], 0.0)
@@ -174,7 +191,7 @@ def tile_akgcn_pb_kernel(tc, x, hid, adj, lam_raw, theta_words, theta_scales, ou
                     )
             target = hid_grouped[u][:, j, :].bitcast(F32).rearrange("p (g n pair) -> p g n pair", g=GROUPS, pair=2)
             source = flipped[:].rearrange("p g pair n -> p g n pair")
-            if j == PACK - 1 and u > 0:
+            if (u, j) in FLIP_V:
                 nc.vector.tensor_copy(out=target, in_=source)
             else:
                 nc.scalar.copy(out=target, in_=source)
@@ -214,7 +231,7 @@ def tile_akgcn_pb_kernel(tc, x, hid, adj, lam_raw, theta_words, theta_scales, ou
                         start=(g == 0),
                         stop=(g == GROUPS - 1),
                     )
-            nc.scalar.copy(
+            (nc.vector.tensor_copy if s in HC_V else nc.scalar.copy)(
                 out=h_grouped[hu][:, BLOCK * quarter : BLOCK * (quarter + 1), :],
                 in_=bank[:].rearrange("p j c -> p c j"),
             )
@@ -253,7 +270,7 @@ def tile_akgcn_pb_kernel(tc, x, hid, adj, lam_raw, theta_words, theta_scales, ou
                 gates[0] = result.tile([P, 2, HALF], F32, name="gate")
             gate = gates[0]
             nc.scalar.activation(out=gate[:, i % 2, :], in_=bank[:], func=ACT.Sigmoid)
-            if s >= STEPS - 2:
+            if s >= SINGLE_FROM:
                 first, count = i, 1
             elif i % 2 == 1:
                 first, count = i - 1, 2

@@ -27,9 +27,14 @@ STEPS_PER_BATCH = T * STEPS_PER_UNIT
 LAG = 6
 HC_V = (25, 29)
 FLIP_V = ((1, 3), (2, 3), (3, 3))
-SINGLE_FROM = 28
+GROUP_OF = (2, 2, 2, 2, 2, 2, 1, 1)
+LAST_SPLIT = 1
+GATE_BUFS = 6
+TOTAL_BUFS = 10
 ADJ_PIECES = 1
 WARM = 0
+V1_AT = 8
+ADJ1_EARLY = False
 
 FLOPS = 2 * UNITS * NODES * CH * CH + 2 * UNITS * NODES * NODES * CH
 
@@ -90,8 +95,11 @@ def tile_akgcn_pb_kernel(tc, x, hid, adj, lam_raw, theta_words, theta_scales, ou
                     .bitcast(I32),
                 )
         load_hid(1)
+        if ADJ1_EARLY:
+            load_adj(1)
         load_x(0)
-        load_adj(1)
+        if not ADJ1_EARLY:
+            load_adj(1)
         load_hid(2)
         load_x(1)
         load_hid(3)
@@ -266,29 +274,33 @@ def tile_akgcn_pb_kernel(tc, x, hid, adj, lam_raw, theta_words, theta_scales, ou
                 start=True,
                 stop=True,
             )
-            if i % 2 == 0:
-                gates[0] = result.tile([P, 2, HALF], F32, name="gate")
+            group = GROUP_OF[hu]
+            if i % group == 0:
+                gates[0] = result.tile([P, group, HALF], F32, name="gate", bufs=GATE_BUFS)
             gate = gates[0]
-            nc.scalar.activation(out=gate[:, i % 2, :], in_=bank[:], func=ACT.Sigmoid)
-            if s >= SINGLE_FROM:
-                first, count = i, 1
-            elif i % 2 == 1:
-                first, count = i - 1, 2
-            else:
-                return
-            total = result.tile([P, 2, HALF], F32, name="total")
-            nc.vector.scalar_tensor_tensor(
-                out=total[:, 0:count, :],
-                in0=gate[:, first % 2 : first % 2 + count, :],
-                scalar=0.5,
-                in1=x_sb[u][:, first : first + count, channels],
-                op0=ALU.max,
-                op1=ALU.add,
-            )
-            nc.sync.dma_start(
-                out=out[u // T, u % T].rearrange("(p i) c -> p i c", i=PACK)[:, first : first + count, channels],
-                in_=total[:, 0:count, :],
-            )
+            pieces = LAST_SPLIT if s == STEPS - 1 else 1
+            width = HALF // pieces
+            for piece in range(pieces):
+                columns = slice(width * piece, width * (piece + 1))
+                nc.scalar.activation(out=gate[:, i % group, columns], in_=bank[:, columns], func=ACT.Sigmoid)
+                if i % group < group - 1:
+                    continue
+                first = i + 1 - group
+                total = result.tile([P, group, HALF], F32, name="total", bufs=TOTAL_BUFS)
+                nc.vector.scalar_tensor_tensor(
+                    out=total[:, :, columns],
+                    in0=gate[:, :, columns],
+                    scalar=0.5,
+                    in1=x_sb[u][:, first : i + 1, HALF * half + width * piece : HALF * half + width * (piece + 1)],
+                    op0=ALU.max,
+                    op1=ALU.add,
+                )
+                nc.sync.dma_start(
+                    out=out[u // T, u % T].rearrange("(p i) c -> p i c", i=PACK)[
+                        :, first : i + 1, HALF * half + width * piece : HALF * half + width * (piece + 1)
+                    ],
+                    in_=total[:, :, columns],
+                )
 
         for j in range(PACK):
             sum_v_rows(0, j)
@@ -307,7 +319,7 @@ def tile_akgcn_pb_kernel(tc, x, hid, adj, lam_raw, theta_words, theta_scales, ou
                     flip_hid(next_unit, j)
                 quantise_hid_whole(next_unit)
             next_batch = s // STEPS_PER_BATCH + 1
-            row = s % STEPS_PER_BATCH - STEPS_PER_UNIT
+            row = s % STEPS_PER_BATCH - V1_AT
             if 0 <= row < PACK and next_batch < B:
                 sum_v_rows(next_batch, row)
             if row == PACK and next_batch < B:

@@ -25,14 +25,19 @@ STEPS_PER_HALF = HALF // BLOCK
 STEPS_PER_UNIT = CH // BLOCK
 STEPS_PER_BATCH = T * STEPS_PER_UNIT
 LAG = 6
-HC_V = (25, 29)
-FLIP_V = ((1, 3), (2, 3), (3, 3))
+HC_V = (1, 2, 25, 29, 30)
+FLIP_V = ((3, 3),)
 GROUP_OF = (2, 2, 2, 2, 2, 2, 1, 1)
 LAST_SPLIT = 1
 GATE_BUFS = 6
 TOTAL_BUFS = 10
 ADJ_PIECES = 1
 WARM = 0
+KEEP_WARM = False
+SCALE0_V = ()
+FLIP_AT = 4
+RELU_PIECES = (1, 1, 1, 1)
+SIGMOID_FIRST = True
 V1_AT = 8
 ADJ1_EARLY = False
 
@@ -154,7 +159,7 @@ def tile_akgcn_pb_kernel(tc, x, hid, adj, lam_raw, theta_words, theta_scales, ou
 
         def scale_v_rows(b, i):
             scaled_rows[(b, i)] = rows.tile([P, PACK, P], BF16, name="scaled")
-            if b == 0:
+            if b == 0 and i not in SCALE0_V:
                 nc.scalar.activation(
                     out=scaled_rows[(b, i)][:], in_=unscaled_rows[(b, i)][:], func=ACT.Copy, scale=inverses[b][:, i : i + 1]
                 )
@@ -222,6 +227,8 @@ def tile_akgcn_pb_kernel(tc, x, hid, adj, lam_raw, theta_words, theta_scales, ou
         h_codes = {}
         h_planes = {}
 
+        h_banks = {}
+
         def first_matmul(s):
             u, block = divmod(s, STEPS_PER_UNIT)
             hu, quarter = divmod(s, STEPS_PER_HALF)
@@ -239,9 +246,15 @@ def tile_akgcn_pb_kernel(tc, x, hid, adj, lam_raw, theta_words, theta_scales, ou
                         start=(g == 0),
                         stop=(g == GROUPS - 1),
                     )
+            h_banks[s] = bank
+            if not SIGMOID_FIRST:
+                empty_h_bank(s)
+
+        def empty_h_bank(s):
+            hu, quarter = divmod(s, STEPS_PER_HALF)
             (nc.vector.tensor_copy if s in HC_V else nc.scalar.copy)(
                 out=h_grouped[hu][:, BLOCK * quarter : BLOCK * (quarter + 1), :],
-                in_=bank[:].rearrange("p j c -> p c j"),
+                in_=h_banks[s][:].rearrange("p j c -> p c j"),
             )
 
         def quantise_h(hu):
@@ -254,8 +267,10 @@ def tile_akgcn_pb_kernel(tc, x, hid, adj, lam_raw, theta_words, theta_scales, ou
             )
 
         def relu_x(u):
-            flat = x_sb[u][:].rearrange("p i c -> p (i c)")
-            nc.vector.tensor_scalar_max(out=flat, in0=flat, scalar1=0.0)
+            width = PACK * CH // RELU_PIECES[u]
+            for piece in range(RELU_PIECES[u]):
+                flat = x_sb[u][:].rearrange("p i c -> p (i c)")[:, width * piece : width * (piece + 1)]
+                nc.vector.tensor_scalar_max(out=flat, in0=flat, scalar1=0.0)
 
         gates = [None]
 
@@ -307,6 +322,8 @@ def tile_akgcn_pb_kernel(tc, x, hid, adj, lam_raw, theta_words, theta_scales, ou
             invert_row_sums(0, j, 1)
             scale_v_rows(0, j)
             flip_hid(0, j)
+            if KEEP_WARM:
+                nc.tensor.matmul(out=idle_bank[:], lhsT=ident_bf, rhs=hid_sb[0][:, j, 0:HALF], start=True, stop=True)
             if j > 0:
                 quantise_hid(0, j - 1)
         quantise_hid(0, PACK - 1)
@@ -314,7 +331,7 @@ def tile_akgcn_pb_kernel(tc, x, hid, adj, lam_raw, theta_words, theta_scales, ou
 
         for s in range(STEPS + LAG):
             next_unit = s // STEPS_PER_UNIT + 1
-            if s % STEPS_PER_UNIT == STEPS_PER_HALF and next_unit < UNITS:
+            if s % STEPS_PER_UNIT == FLIP_AT and next_unit < UNITS:
                 for j in range(PACK):
                     flip_hid(next_unit, j)
                 quantise_hid_whole(next_unit)
@@ -334,5 +351,7 @@ def tile_akgcn_pb_kernel(tc, x, hid, adj, lam_raw, theta_words, theta_scales, ou
                 first_matmul(s)
             if s >= LAG:
                 second_matmul(s - LAG)
+            if SIGMOID_FIRST and s < STEPS:
+                empty_h_bank(s)
             if s < STEPS and s % STEPS_PER_HALF == STEPS_PER_HALF - 1:
                 quantise_h(s // STEPS_PER_HALF)

@@ -24,7 +24,7 @@ STEPS = UNITS * CH // BLOCK
 STEPS_PER_HALF = HALF // BLOCK
 STEPS_PER_UNIT = CH // BLOCK
 STEPS_PER_BATCH = T * STEPS_PER_UNIT
-LAG = 6
+LAG = 7
 HC_V = (1, 2, 25, 29, 30)
 FLIP_V = ((3, 3),)
 GROUP_OF = (2, 2, 2, 2, 2, 2, 1, 1)
@@ -38,8 +38,11 @@ SCALE0_V = ()
 FLIP_AT = 4
 RELU_PIECES = (1, 1, 1, 1)
 SIGMOID_FIRST = True
+PIN_TENSOR = False
+H_GROUPED_BUFS = 3
+H_CODES_BUFS = 4
 V1_AT = 8
-ADJ1_EARLY = False
+ADJ1_EARLY = 0
 
 FLOPS = 2 * UNITS * NODES * CH * CH + 2 * UNITS * NODES * NODES * CH
 
@@ -53,6 +56,8 @@ def tile_akgcn_pb_kernel(tc, x, hid, adj, lam_raw, theta_words, theta_scales, ou
         stage = stack.enter_context(tc.tile_pool(name="stage", bufs=2))
         result = stack.enter_context(tc.tile_pool(name="result", bufs=6))
         banks = stack.enter_context(tc.psum_pool(name="banks", bufs=8))
+        if PIN_TENSOR:
+            stack.enter_context(tc.manual_schedule(engines={mybir.EngineType.PE}))
 
         lam_bf = keep.tile([P, 1], BF16, name="lam_bf")
         adj_sb = [keep.tile([P, PACK, NODES], BF16, name="adj%d" % b) for b in range(B)]
@@ -99,8 +104,10 @@ def tile_akgcn_pb_kernel(tc, x, hid, adj, lam_raw, theta_words, theta_scales, ou
                     .rearrange("p n t -> p (n t)")
                     .bitcast(I32),
                 )
+        if ADJ1_EARLY == 2:
+            load_adj(1)
         load_hid(1)
-        if ADJ1_EARLY:
+        if ADJ1_EARLY == 1:
             load_adj(1)
         load_x(0)
         if not ADJ1_EARLY:
@@ -233,7 +240,7 @@ def tile_akgcn_pb_kernel(tc, x, hid, adj, lam_raw, theta_words, theta_scales, ou
             u, block = divmod(s, STEPS_PER_UNIT)
             hu, quarter = divmod(s, STEPS_PER_HALF)
             if quarter == 0:
-                h_grouped[hu] = stage.tile([P, HALF, PACK], BF16, name="h_grouped", align_bytes=64)
+                h_grouped[hu] = stage.tile([P, HALF, PACK], BF16, name="h_grouped", align_bytes=64, bufs=H_GROUPED_BUFS)
             bank = banks.tile([P, PACK, BLOCK], F32, name="h_bank", tag="bank")
             for j in range(PACK):
                 for g in range(GROUPS):
@@ -258,8 +265,8 @@ def tile_akgcn_pb_kernel(tc, x, hid, adj, lam_raw, theta_words, theta_scales, ou
             )
 
         def quantise_h(hu):
-            h_codes[hu] = stage.tile([P, HALF], U32, name="h_codes", align_bytes=64, bufs=3)
-            h_planes[hu] = stage.tile([P, HALF], U8, name="h_planes", align_bytes=64, bufs=3)
+            h_codes[hu] = stage.tile([P, HALF], U32, name="h_codes", align_bytes=64, bufs=H_CODES_BUFS)
+            h_planes[hu] = stage.tile([P, HALF], U8, name="h_planes", align_bytes=64, bufs=H_CODES_BUFS)
             nc.vector.quantize_mx(
                 out=h_codes[hu][:].bitcast(FP8X4),
                 scales=h_planes[hu][:],

@@ -25,8 +25,8 @@ STEPS_PER_HALF = HALF // BLOCK
 STEPS_PER_UNIT = CH // BLOCK
 STEPS_PER_BATCH = T * STEPS_PER_UNIT
 LAG = 7
-HC_V = (1, 2, 25, 29, 30)
-FLIP_V = ((3, 3),)
+HC_V = (1, 2, 25, 29)
+FLIP_V = ()
 GROUP_OF = (2, 2, 2, 2, 2, 2, 1, 1)
 LAST_SPLIT = 1
 GATE_BUFS = 6
@@ -36,9 +36,11 @@ WARM = 0
 KEEP_WARM = False
 SCALE0_V = ()
 FLIP_AT = 4
+FLIP_AT_LATER = 4
 RELU_PIECES = (1, 1, 1, 1)
 SIGMOID_FIRST = True
 PIN_TENSOR = False
+Z_PAIR_BUFS = 0
 H_GROUPED_BUFS = 3
 H_CODES_BUFS = 4
 V1_AT = 8
@@ -55,7 +57,9 @@ def tile_akgcn_pb_kernel(tc, x, hid, adj, lam_raw, theta_words, theta_scales, ou
         rows = stack.enter_context(tc.tile_pool(name="rows", bufs=4))
         stage = stack.enter_context(tc.tile_pool(name="stage", bufs=2))
         result = stack.enter_context(tc.tile_pool(name="result", bufs=6))
-        banks = stack.enter_context(tc.psum_pool(name="banks", bufs=8))
+        banks = stack.enter_context(tc.psum_pool(name="banks", bufs=8 - 2 * Z_PAIR_BUFS))
+        if Z_PAIR_BUFS:
+            double_banks = stack.enter_context(tc.psum_pool(name="double_banks", bufs=Z_PAIR_BUFS))
         if PIN_TENSOR:
             stack.enter_context(tc.manual_schedule(engines={mybir.EngineType.PE}))
 
@@ -280,15 +284,22 @@ def tile_akgcn_pb_kernel(tc, x, hid, adj, lam_raw, theta_words, theta_scales, ou
                 nc.vector.tensor_scalar_max(out=flat, in0=flat, scalar1=0.0)
 
         gates = [None]
+        z_pairs = [None]
 
         def second_matmul(s):
             hu, i = divmod(s, STEPS_PER_HALF)
             u, half = divmod(hu, 2)
             b = u // T
             channels = slice(HALF * half, HALF * (half + 1))
-            bank = banks.tile([P, HALF], F32, name="z_bank", tag="bank")
+            group = GROUP_OF[hu]
+            if Z_PAIR_BUFS:
+                if i % 2 == 0:
+                    z_pairs[0] = double_banks.tile([P, 2, HALF], F32, name="z_pair")
+                bank = z_pairs[0][:, i % 2, :]
+            else:
+                bank = banks.tile([P, HALF], F32, name="z_bank", tag="bank")[:]
             nc.tensor.matmul_mx(
-                out=bank[:],
+                out=bank,
                 lhsT=v_codes[b][:, P * i : P * (i + 1)].bitcast(FP8X4),
                 lhsT_scale=v_planes[b][:, P * i : P * (i + 1)],
                 rhs=h_codes[hu][:].bitcast(FP8X4),
@@ -296,7 +307,6 @@ def tile_akgcn_pb_kernel(tc, x, hid, adj, lam_raw, theta_words, theta_scales, ou
                 start=True,
                 stop=True,
             )
-            group = GROUP_OF[hu]
             if i % group == 0:
                 gates[0] = result.tile([P, group, HALF], F32, name="gate", bufs=GATE_BUFS)
             gate = gates[0]
@@ -304,7 +314,11 @@ def tile_akgcn_pb_kernel(tc, x, hid, adj, lam_raw, theta_words, theta_scales, ou
             width = HALF // pieces
             for piece in range(pieces):
                 columns = slice(width * piece, width * (piece + 1))
-                nc.scalar.activation(out=gate[:, i % group, columns], in_=bank[:, columns], func=ACT.Sigmoid)
+                if Z_PAIR_BUFS and group == 2:
+                    if i % 2 == 1:
+                        nc.scalar.activation(out=gate[:], in_=z_pairs[0][:], func=ACT.Sigmoid)
+                else:
+                    nc.scalar.activation(out=gate[:, i % group, columns], in_=bank[:, columns], func=ACT.Sigmoid)
                 if i % group < group - 1:
                     continue
                 first = i + 1 - group
@@ -338,7 +352,7 @@ def tile_akgcn_pb_kernel(tc, x, hid, adj, lam_raw, theta_words, theta_scales, ou
 
         for s in range(STEPS + LAG):
             next_unit = s // STEPS_PER_UNIT + 1
-            if s % STEPS_PER_UNIT == FLIP_AT and next_unit < UNITS:
+            if s % STEPS_PER_UNIT == (FLIP_AT if next_unit == 1 else FLIP_AT_LATER) and next_unit < UNITS:
                 for j in range(PACK):
                     flip_hid(next_unit, j)
                 quantise_hid_whole(next_unit)

from contextlib import ExitStack

import concourse.mybir as mybir
from concourse.masks import make_identity

F32 = mybir.dt.float32
BF16 = mybir.dt.bfloat16
I32 = mybir.dt.int32
U32 = mybir.dt.uint32
U8 = mybir.dt.uint8
FP8X4 = mybir.dt.float8_e4m3fn_x4
ALU = mybir.AluOpType
ACT = mybir.ActivationFunctionType

B, T, NODES, CH = 2, 2, 512, 1024
P = 128
PACK = 4
K_PASS = P * PACK
UNITS = B * T
GROUPS = CH // K_PASS
HALF = CH // 2
BLOCK = P
STEPS = UNITS * CH // BLOCK
STEPS_PER_HALF = HALF // BLOCK
STEPS_PER_UNIT = CH // BLOCK
STEPS_PER_BATCH = T * STEPS_PER_UNIT
LAG = 7
HC_V = (1, 2, 25, 29)
FLIP_V = ()
GROUP_OF = (2, 2, 2, 2, 2, 2, 1, 1)
LAST_SPLIT = 1
GATE_BUFS = 6
TOTAL_BUFS = 10
ADJ_PIECES = 1
WARM = 0
KEEP_WARM = False
SCALE0_V = ()
FLIP_AT = 4
FLIP_AT_LATER = 4
RELU_PIECES = (1, 1, 1, 1)
SIGMOID_FIRST = True
PIN_TENSOR = False
Z_PAIR_BUFS = 0
H_GROUPED_BUFS = 3
H_CODES_BUFS = 4
V1_AT = 8
ADJ1_EARLY = 0

FLOPS = 2 * UNITS * NODES * CH * CH + 2 * UNITS * NODES * NODES * CH


def tile_akgcn_pb_kernel(tc, x, hid, adj, lam_raw, theta_words, theta_scales, out):
    nc = tc.nc
    with ExitStack() as stack:
        keep = stack.enter_context(tc.tile_pool(name="keep", bufs=1))
        small = stack.enter_context(tc.tile_pool(name="small", bufs=4))
        rows = stack.enter_context(tc.tile_pool(name="rows", bufs=4))
        stage = stack.enter_context(tc.tile_pool(name="stage", bufs=2))
        result = stack.enter_context(tc.tile_pool(name="result", bufs=6))
        banks = stack.enter_context(tc.psum_pool(name="banks", bufs=8 - 2 * Z_PAIR_BUFS))
        if Z_PAIR_BUFS:
            double_banks = stack.enter_context(tc.psum_pool(name="double_banks", bufs=Z_PAIR_BUFS))
        if PIN_TENSOR:
            stack.enter_context(tc.manual_schedule(engines={mybir.EngineType.PE}))

        lam_bf = keep.tile([P, 1], BF16, name="lam_bf")
        adj_sb = [keep.tile([P, PACK, NODES], BF16, name="adj%d" % b) for b in range(B)]
        hid_sb = [keep.tile([P, PACK, CH], BF16, name="hid%d" % u) for u in range(UNITS)]
        x_sb = [keep.tile([P, PACK, CH], BF16, name="x%d" % u) for u in range(UNITS)]
        theta_codes = keep.tile([P, GROUPS, CH], U32, name="theta_codes", align_bytes=64)
        theta_planes = keep.tile([P, GROUPS, CH], U8, name="theta_planes", align_bytes=64)
        v_codes = [keep.tile([P, NODES], U32, name="v_codes%d" % b, align_bytes=64) for b in range(B)]
        v_planes = [keep.tile([P, NODES], U8, name="v_planes%d" % b, align_bytes=64) for b in range(B)]

        nc.vector.memset(theta_planes[:].bitcast(I32), 0)

        nc.sync.dma_start(out=lam_bf[:], in_=lam_raw.partition_broadcast(P))

        def load_adj(b):
            nc.sync.dma_start(out=adj_sb[b][:], in_=adj[b].rearrange("(p i) m -> p i m", i=PACK))

        def load_hid(u):
            nc.sync.dma_start(out=hid_sb[u][:], in_=hid[u // T, u % T].rearrange("(p j) k -> p j k", j=PACK))

        def load_x(u):
            nc.sync.dma_start(out=x_sb[u][:], in_=x[u // T, u % T].rearrange("(p i) c -> p i c", i=PACK))

        for piece in range(ADJ_PIECES):
            span = PACK // ADJ_PIECES
            nc.sync.dma_start(
                out=adj_sb[0][:, span * piece : span * (piece + 1), :],
                in_=adj[0].rearrange("(p i) m -> p i m", i=PACK)[:, span * piece : span * (piece + 1), :],
            )
        for j in range(PACK):
            nc.sync.dma_start(
                out=hid_sb[0][:, j, :], in_=hid[0, 0].rearrange("(p j) k -> p j k", j=PACK)[:, j, :]
            )
        for quadrant in range(4):
            nc.sync.dma_start(
                out=theta_planes[32 * quadrant : 32 * quadrant + 4, :, :].bitcast(I32),
                in_=theta_scales[:, 4 * quadrant : 4 * quadrant + 4, :].rearrange("g r n -> r g n").bitcast(I32),
            )
        for half in range(2):
            for g in range(GROUPS):
                nc.sync.dma_start(
                    out=theta_codes[:, g, HALF * half : HALF * (half + 1)].bitcast(I32),
                    in_=theta_words[g, :, HALF * half : HALF * (half + 1), :]
                    .rearrange("p n t -> p (n t)")
                    .bitcast(I32),
                )
        if ADJ1_EARLY == 2:
            load_adj(1)
        load_hid(1)
        if ADJ1_EARLY == 1:
            load_adj(1)
        load_x(0)
        if not ADJ1_EARLY:
            load_adj(1)
        load_hid(2)
        load_x(1)
        load_hid(3)
        load_x(2)
        load_x(3)

        eye_strip = keep.tile([P, 2 * PACK - 1, P], BF16, name="eye_strip")
        nc.gpsimd.memset(eye_strip[:], 0.0)
        make_identity(nc, eye_strip[:, PACK - 1, :])
        ident_bf = eye_strip[:, PACK - 1, :]
        ident_f32 = keep.tile([P, P], F32, name="ident_f32")
        make_identity(nc, ident_f32[:])

        if WARM:
            idle_rows = keep.tile([P, HALF], BF16, name="idle_rows")
            nc.vector.memset(idle_rows[:], 0.0)
            idle_bank = banks.tile([P, HALF], F32, name="idle_bank", tag="bank")
            for repeat in range(WARM):
                nc.tensor.matmul(out=idle_bank[:], lhsT=idle_rows[:, 0:P], rhs=idle_rows[:], start=True, stop=True)

        warm = keep.tile([P, 1], F32, name="warm")
        nc.vector.memset(warm[:], 0.0)
        nc.scalar.activation(out=warm[:], in_=warm[:], func=ACT.Sigmoid)

        r = keep.tile([P, 1], F32, name="r")
        nc.vector.tensor_scalar_max(out=r[:], in0=lam_bf[:], scalar1=0.0)

        unscaled_rows = {}
        row_sums = {}

        def sum_v_rows(b, i):
            if i == 0:
                row_sums[b] = small.tile([P, PACK], F32, name="row_sums")
            unscaled_rows[(b, i)] = rows.tile([P, PACK, P], F32, name="unscaled")
            nc.vector.scalar_tensor_tensor(
                out=unscaled_rows[(b, i)][:],
                in0=eye_strip[:, PACK - 1 - i : 2 * PACK - 1 - i, :],
                scalar=r[:, 0:1],
                in1=adj_sb[b][:, i, :].rearrange("p (q t) -> p t q", t=PACK),
                op0=ALU.mult,
                op1=ALU.add,
                accum_out=row_sums[b][:, i : i + 1],
            )

        inverses = {}
        scaled_rows = {}

        def invert_row_sums(b, first, count):
            if first == 0:
                inverses[b] = small.tile([P, PACK], F32, name="inverse")
            nc.vector.reciprocal(out=inverses[b][:, first : first + count], in_=row_sums[b][:, first : first + count])

        def scale_v_rows(b, i):
            scaled_rows[(b, i)] = rows.tile([P, PACK, P], BF16, name="scaled")
            if b == 0 and i not in SCALE0_V:
                nc.scalar.activation(
                    out=scaled_rows[(b, i)][:], in_=unscaled_rows[(b, i)][:], func=ACT.Copy, scale=inverses[b][:, i : i + 1]
                )
            else:
                nc.vector.tensor_scalar_mul(
                    out=scaled_rows[(b, i)][:], in0=unscaled_rows[(b, i)][:], scalar1=inverses[b][:, i : i + 1]
                )

        def transpose_v(b):
            v_grouped = stage.tile([P, PACK, P, PACK], BF16, name="v_grouped", align_bytes=64)
            for pair in range(PACK // 2):
                flipped = banks.tile([P, 2, PACK, P], BF16, name="flipped_v", tag="bank")
                for k in range(2):
                    for t in range(PACK):
                        nc.tensor.transpose(flipped[:, k, t, :], scaled_rows[(b, 2 * pair + k)][:, t, :], ident_bf)
                nc.vector.tensor_copy(
                    out=v_grouped[:, 2 * pair : 2 * pair + 2, :, :], in_=flipped[:].rearrange("q k t p -> q k p t")
                )
            nc.vector.quantize_mx(
                out=v_codes[b][:].bitcast(FP8X4),
                scales=v_planes[b][:],
                in_=v_grouped[:].rearrange("q i p t -> q (i p t)"),
            )

        hid_grouped = {}
        hid_codes = {}
        hid_planes = {}

        def flip_hid(u, j):
            if j == 0:
                hid_grouped[u] = stage.tile([P, PACK, GROUPS * P * PACK], BF16, name="hid_grouped", align_bytes=64)
                hid_codes[u] = stage.tile([P, PACK, GROUPS * P], U32, name="hid_codes", align_bytes=64)
                hid_planes[u] = stage.tile([P, PACK, GROUPS * P], U8, name="hid_planes", align_bytes=64)
            words = hid_sb[u][:, j, :].bitcast(F32)
            flipped = banks.tile([P, GROUPS, 2, P], F32, name="flipped_hid", tag="bank")
            for g in range(GROUPS):
                for pair in range(2):
                    nc.tensor.transpose(
                        flipped[:, g, pair, :],
                        words[:, 256 * g + pair : 256 * (g + 1) : 2],
                        ident_f32[:],
                    )
            target = hid_grouped[u][:, j, :].bitcast(F32).rearrange("p (g n pair) -> p g n pair", g=GROUPS, pair=2)
            source = flipped[:].rearrange("p g pair n -> p g n pair")
            if (u, j) in FLIP_V:
                nc.vector.tensor_copy(out=target, in_=source)
            else:
                nc.scalar.copy(out=target, in_=source)

        def quantise_hid(u, j):
            nc.vector.quantize_mx(
                out=hid_codes[u][:, j, :].bitcast(FP8X4),
                scales=hid_planes[u][:, j, :],
                in_=hid_grouped[u][:, j, :],
            )

        def quantise_hid_whole(u):
            nc.vector.quantize_mx(
                out=hid_codes[u][:].rearrange("p j n -> p (j n)").bitcast(FP8X4),
                scales=hid_planes[u][:].rearrange("p j n -> p (j n)"),
                in_=hid_grouped[u][:].rearrange("p j n -> p (j n)"),
            )

        h_grouped = {}
        h_codes = {}
        h_planes = {}

        h_banks = {}

        def first_matmul(s):
            u, block = divmod(s, STEPS_PER_UNIT)
            hu, quarter = divmod(s, STEPS_PER_HALF)
            if quarter == 0:
                h_grouped[hu] = stage.tile([P, HALF, PACK], BF16, name="h_grouped", align_bytes=64, bufs=H_GROUPED_BUFS)
            bank = banks.tile([P, PACK, BLOCK], F32, name="h_bank", tag="bank")
            for j in range(PACK):
                for g in range(GROUPS):
                    nc.tensor.matmul_mx(
                        out=bank[:, j, :],
                        lhsT=hid_codes[u][:, j, P * g : P * (g + 1)].bitcast(FP8X4),
                        lhsT_scale=hid_planes[u][:, j, P * g : P * (g + 1)],
                        rhs=theta_codes[:, g, BLOCK * block : BLOCK * (block + 1)].bitcast(FP8X4),
                        rhs_scale=theta_planes[:, g, BLOCK * block : BLOCK * (block + 1)],
                        start=(g == 0),
                        stop=(g == GROUPS - 1),
                    )
            h_banks[s] = bank
            if not SIGMOID_FIRST:
                empty_h_bank(s)

        def empty_h_bank(s):
            hu, quarter = divmod(s, STEPS_PER_HALF)
            (nc.vector.tensor_copy if s in HC_V else nc.scalar.copy)(
                out=h_grouped[hu][:, BLOCK * quarter : BLOCK * (quarter + 1), :],
                in_=h_banks[s][:].rearrange("p j c -> p c j"),
            )

        def quantise_h(hu):
            h_codes[hu] = stage.tile([P, HALF], U32, name="h_codes", align_bytes=64, bufs=H_CODES_BUFS)
            h_planes[hu] = stage.tile([P, HALF], U8, name="h_planes", align_bytes=64, bufs=H_CODES_BUFS)
            nc.vector.quantize_mx(
                out=h_codes[hu][:].bitcast(FP8X4),
                scales=h_planes[hu][:],
                in_=h_grouped[hu][:].rearrange("p c j -> p (c j)"),
            )

        def relu_x(u):
            width = PACK * CH // RELU_PIECES[u]
            for piece in range(RELU_PIECES[u]):
                flat = x_sb[u][:].rearrange("p i c -> p (i c)")[:, width * piece : width * (piece + 1)]
                nc.vector.tensor_scalar_max(out=flat, in0=flat, scalar1=0.0)

        gates = [None]
        z_pairs = [None]

        def second_matmul(s):
            hu, i = divmod(s, STEPS_PER_HALF)
            u, half = divmod(hu, 2)
            b = u // T
            channels = slice(HALF * half, HALF * (half + 1))
            group = GROUP_OF[hu]
            if Z_PAIR_BUFS:
                if i % 2 == 0:
                    z_pairs[0] = double_banks.tile([P, 2, HALF], F32, name="z_pair")
                bank = z_pairs[0][:, i % 2, :]
            else:
                bank = banks.tile([P, HALF], F32, name="z_bank", tag="bank")[:]
            nc.tensor.matmul_mx(
                out=bank,
                lhsT=v_codes[b][:, P * i : P * (i + 1)].bitcast(FP8X4),
                lhsT_scale=v_planes[b][:, P * i : P * (i + 1)],
                rhs=h_codes[hu][:].bitcast(FP8X4),
                rhs_scale=h_planes[hu][:],
                start=True,
                stop=True,
            )
            if i % group == 0:
                gates[0] = result.tile([P, group, HALF], F32, name="gate", bufs=GATE_BUFS)
            gate = gates[0]
            pieces = LAST_SPLIT if s == STEPS - 1 else 1
            width = HALF // pieces
            for piece in range(pieces):
                columns = slice(width * piece, width * (piece + 1))
                if Z_PAIR_BUFS and group == 2:
                    if i % 2 == 1:
                        nc.scalar.activation(out=gate[:], in_=z_pairs[0][:], func=ACT.Sigmoid)
                else:
                    nc.scalar.activation(out=gate[:, i % group, columns], in_=bank[:, columns], func=ACT.Sigmoid)
                if i % group < group - 1:
                    continue
                first = i + 1 - group
                total = result.tile([P, group, HALF], F32, name="total", bufs=TOTAL_BUFS)
                nc.vector.scalar_tensor_tensor(
                    out=total[:, :, columns],
                    in0=gate[:, :, columns],
                    scalar=0.5,
                    in1=x_sb[u][:, first : i + 1, HALF * half + width * piece : HALF * half + width * (piece + 1)],
                    op0=ALU.max,
                    op1=ALU.add,
                )
                nc.sync.dma_start(
                    out=out[u // T, u % T].rearrange("(p i) c -> p i c", i=PACK)[
                        :, first : i + 1, HALF * half + width * piece : HALF * half + width * (piece + 1)
                    ],
                    in_=total[:, :, columns],
                )

        for j in range(PACK):
            sum_v_rows(0, j)
            invert_row_sums(0, j, 1)
            scale_v_rows(0, j)
            flip_hid(0, j)
            if KEEP_WARM:
                nc.tensor.matmul(out=idle_bank[:], lhsT=ident_bf, rhs=hid_sb[0][:, j, 0:HALF], start=True, stop=True)
            if j > 0:
                quantise_hid(0, j - 1)
        quantise_hid(0, PACK - 1)
        transpose_v(0)

        for s in range(STEPS + LAG):
            next_unit = s // STEPS_PER_UNIT + 1
            if s % STEPS_PER_UNIT == (FLIP_AT if next_unit == 1 else FLIP_AT_LATER) and next_unit < UNITS:
                for j in range(PACK):
                    flip_hid(next_unit, j)
                quantise_hid_whole(next_unit)
            next_batch = s // STEPS_PER_BATCH + 1
            row = s % STEPS_PER_BATCH - V1_AT
            if 0 <= row < PACK and next_batch < B:
                sum_v_rows(next_batch, row)
            if row == PACK and next_batch < B:
                invert_row_sums(next_batch, 0, PACK)
            if PACK <= row < 2 * PACK and next_batch < B:
                scale_v_rows(next_batch, row - PACK)
            if s % STEPS_PER_BATCH == 0 and 0 < s < STEPS:
                transpose_v(s // STEPS_PER_BATCH)
            if (s + 1 - LAG) % STEPS_PER_UNIT == 0 and s + 1 - LAG < STEPS:
                relu_x((s + 1 - LAG) // STEPS_PER_UNIT)
            if s < STEPS:
                first_matmul(s)
            if s >= LAG:
                second_matmul(s - LAG)
            if SIGMOID_FIRST and s < STEPS:
                empty_h_bank(s)
            if s < STEPS and s % STEPS_PER_HALF == STEPS_PER_HALF - 1:
                quantise_h(s // STEPS_PER_HALF)
